import numpy as np
import ml_dtypes


def mxq(x, axis, fmt="e4m3"):
    dtype, down = {"e4m3": (ml_dtypes.float8_e4m3fn, 7), "e5m2": (ml_dtypes.float8_e5m2, 14)}[fmt]
    v = np.moveaxis(np.asarray(x, np.float32).astype(ml_dtypes.bfloat16).astype(np.float64), axis, -1)
    blocks = v.reshape(v.shape[:-1] + (-1, 32))
    amax = np.abs(blocks).max(-1, keepdims=True)
    byte = np.maximum(np.where(amax > 0, np.frexp(amax)[1] - 1 + 127, 0) - down, 1)
    scale = np.exp2(byte - 127.0)
    codes = (blocks / scale).astype(np.float32).astype(dtype).astype(np.float64)
    return np.moveaxis((codes * scale).reshape(v.shape), -1, axis)


WIDE = False


def mx_kscale(k):
    if not WIDE:
        return np.ones(k)
    levels = np.array([10, -10, 5, -5, 0])
    a = np.random.permutation(np.resize(levels, k // 512 * 4)).reshape(k // 512, 4)
    idx = np.arange(k)
    return np.exp2(a[idx // 512, idx % 128 // 32])


BF16 = ml_dtypes.bfloat16


def bf(x):
    return np.asarray(x, np.float32).astype(BF16)


def f64(x):
    return np.asarray(x).astype(np.float64)


N, D, O, H, W = 6, 512, 128, 32, 32
K = D + D
P = H * W


def sigmoid(v):
    return 1.0 / (1.0 + np.exp(-v))


def spatial_gate(re, x_orig):
    a = np.exp(re)
    e = np.exp(a - a.max(1, keepdims=True))
    sm = e / e.sum(1, keepdims=True)
    s = (sm * re).sum(1, keepdims=True)
    return x_orig * s


def setup_inputs():
    t = mx_kscale(D)
    u = t / t.max()
    uc = u[None, :, None, None]
    uu = np.concatenate([u, u])
    return {"x1": bf(np.random.standard_normal((N, D, H, W)) * 0.5 * uc), "x2": bf(np.random.standard_normal((N, D, H, W)) * 0.5 * uc),
            "FE_x1": bf(np.random.standard_normal((N, D, H, W)) * 0.5 * uc), "FE_x2": bf(np.random.standard_normal((N, D, H, W)) * 0.5 * uc),
            "g1": bf(np.random.standard_normal((N, D)) * 1.2), "g2": bf(np.random.standard_normal((N, D)) * 1.2),
            "p1_w": bf(np.random.standard_normal((O, K)) / np.sqrt(K) / uu), "p1_b": bf(np.random.standard_normal(O) * 0.3),
            "p2_w": bf(np.random.standard_normal((O, K)) / np.sqrt(K) / uu), "p2_b": bf(np.random.standard_normal(O) * 0.3)}


def reference(x1, x2, FE_x1, FE_x2, g1, g2, p1_w, p1_b, p2_w, p2_b):
    a1 = f64(x1).reshape(N, D, P)
    a2 = f64(x2).reshape(N, D, P)
    re_x1 = a1 * sigmoid(f64(g1))[:, :, None] + a2
    re_x2 = a2 * sigmoid(f64(g2))[:, :, None] + a1
    fg_x1_sp = spatial_gate(re_x1, a1) + a2
    fg_x2_sp = spatial_gate(re_x2, a2) + a1
    co_x1 = fg_x1_sp + f64(FE_x1).reshape(N, D, P)
    co_x2 = fg_x2_sp + f64(FE_x2).reshape(N, D, P)
    re = np.concatenate([co_x1, co_x2], axis=1)
    rq = mxq(re, 1, "e4m3")
    po_x1 = (mxq(f64(p1_w), 1, "e4m3") @ rq) + f64(p1_b)[None, :, None]
    po_x2 = (mxq(f64(p2_w), 1, "e4m3") @ rq) + f64(p2_b)[None, :, None]
    return po_x1.reshape(N, O, H, W), po_x2.reshape(N, O, H, W)

@@ -1,0 +1,172 @@
+from contextlib import ExitStack
+
+import concourse.mybir as mybir
+from concourse.masks import make_identity
+
+F32 = mybir.dt.float32
+BF16 = mybir.dt.bfloat16
+U32 = mybir.dt.uint32
+U8 = mybir.dt.uint8
+FP8X4 = mybir.dt.float8_e4m3fn_x4
+ALU = mybir.AluOpType
+ACT = mybir.ActivationFunctionType
+
+P = 128
+PACK = 4
+IMAGES = 6
+D = 512
+CHUNKS = D // P
+POS = 1024
+HALF = 512
+BLOCKS = HALF // P
+STREAMS = 2
+OUT = 128
+
+FLOPS = 2 * (2 * OUT) * (STREAMS * D) * (IMAGES * POS)
+
+
+def tile_fr_pb_t_kernel(tc, x1, x2, FE_x1, FE_x2, g1, g2, p1_w, p1_b, p2_w, p2_b, out_0, out_1):
+    nc = tc.nc
+    map_views = [m.rearrange("n (j p) h w -> n p j (h w)", p=P) for m in (x1, x2, FE_x1, FE_x2)]
+    out_views = [o.rearrange("n o h w -> n o (h w)") for o in (out_0, out_1)]
+
+    with ExitStack() as ctx:
+        const = ctx.enter_context(tc.tile_pool(name="const", bufs=1))
+        loads = ctx.enter_context(tc.tile_pool(name="loads", bufs=3))
+        work = ctx.enter_context(tc.tile_pool(name="work", bufs=2))
+        stats = ctx.enter_context(tc.tile_pool(name="stats", bufs=4))
+        psum = ctx.enter_context(tc.psum_pool(name="psum", bufs=1))
+
+        ident_f32 = const.tile([P, P], F32)
+        make_identity(nc, ident_f32[:])
+        ident_bf16 = const.tile([P, P], BF16)
+        make_identity(nc, ident_bf16[:])
+
+        rows = const.tile([P, P], BF16)
+        nc.vector.memset(rows[:], 0.0)
+        nc.sync.dma_start(out=rows[0:24, :], in_=g1.rearrange("n (j p) -> (n j) p", p=P))
+        nc.sync.dma_start(out=rows[24:48, :], in_=g2.rearrange("n (j p) -> (n j) p", p=P))
+        nc.sync.dma_start(out=rows[48:49, :], in_=p1_b.rearrange("(o p) -> o p", o=1))
+        nc.sync.dma_start(out=rows[49:50, :], in_=p2_b.rearrange("(o p) -> o p", o=1))
+        columns = psum.tile([P, P], BF16, tag="xT")
+        nc.tensor.transpose(columns[:], rows[:], ident_bf16[:])
+        gate = const.tile([P, STREAMS * IMAGES * CHUNKS], F32)
+        nc.scalar.activation(out=gate[:], in_=columns[:, 0:48], func=ACT.Sigmoid)
+        bias = const.tile([P, 2], F32)
+        nc.vector.tensor_copy(out=bias[:], in_=columns[:, 48:50])
+
+        w_grouped = const.tile([P, 2, STREAMS, OUT, PACK], BF16, align_bytes=64)
+        for w, weight in enumerate((p1_w, p2_w)):
+            w_raw = const.tile([P, STREAMS * D], BF16, tag="w_raw%d" % w)
+            nc.sync.dma_start(out=w_raw[:], in_=weight)
+            wT = psum.tile([P, STREAMS, PACK, OUT], BF16, tag="xT")
+            for i in range(STREAMS):
+                for t in range(PACK):
+                    k0 = D * i + P * t
+                    nc.tensor.transpose(wT[:, i, t, :], w_raw[:, k0 : k0 + P], ident_bf16[:])
+            nc.vector.tensor_copy(out=w_grouped[:, w], in_=wT[:].rearrange("p i t o -> p i o t"))
+        w_codes = const.tile([P, 2 * STREAMS * OUT], U32, align_bytes=64)
+        w_scales = const.tile([P, 2 * STREAMS * OUT], U8, align_bytes=64)
+        nc.vector.quantize_mx(
+            out=w_codes[:].bitcast(FP8X4),
+            scales=w_scales[:],
+            in_=w_grouped[:].rearrange("p w i o t -> p (w i o t)"),
+        )
+
+        for n in range(IMAGES):
+            maps = []
+            for which in range(4):
+                loaded = loads.tile([P, CHUNKS, POS], BF16, tag="map%d" % which)
+                nc.sync.dma_start(out=loaded[:], in_=map_views[which][n])
+                maps.append(loaded)
+
+            for half in range(POS // HALF):
+                first = half * HALF
+                cols = slice(first, first + HALF)
+                codes = work.tile([P, STREAMS, HALF], U32, align_bytes=64)
+                scales = work.tile([P, STREAMS, HALF], U8, align_bytes=64)
+
+                for i in range(STREAMS):
+                    own, other, extra = maps[i], maps[1 - i], maps[2 + i]
+
+                    r = work.tile([P, CHUNKS, HALF], F32)
+                    for j in range(CHUNKS):
+                        g_col = (i * IMAGES + n) * CHUNKS + j
+                        nc.vector.scalar_tensor_tensor(
+                            out=r[:, j, :],
+                            in0=own[:, j, cols],
+                            scalar=gate[:, g_col : g_col + 1],
+                            in1=other[:, j, cols],
+                            op0=ALU.mult,
+                            op1=ALU.add,
+                        )
+                    u = work.tile([P, CHUNKS, HALF], F32)
+                    nc.gpsimd.tensor_tensor(out=u[:], in0=other[:, :, cols], in1=extra[:, :, cols], op=ALU.add)
+
+                    sum_e = stats.tile([P, BLOCKS], F32)
+                    sum_er = stats.tile([P, BLOCKS], F32)
+                    for b in range(BLOCKS):
+                        rT = psum.tile([P, D], F32, tag="rT", bufs=3)
+                        for j in range(CHUNKS):
+                            nc.tensor.transpose(rT[:, j * P : (j + 1) * P], r[:, j, b * P : (b + 1) * P], ident_f32[:])
+                        e = work.tile([P, D], F32, bufs=4)
+                        nc.scalar.activation(out=e[:], in_=rT[:], func=ACT.Exp)
+                        neg_max = stats.tile([P, 1], F32)
+                        nc.vector.tensor_reduce(
+                            out=neg_max[:], in_=e[:], axis=mybir.AxisListType.X, op=ALU.max, negate=True
+                        )
+                        nc.scalar.activation(
+                            out=e[:], in_=e[:], func=ACT.Exp, bias=neg_max[:], accum_out=sum_e[:, b : b + 1]
+                        )
+                        nc.vector.scalar_tensor_tensor(
+                            out=e[:],
+                            in0=e[:],
+                            scalar=1.0,
+                            in1=rT[:],
+                            op0=ALU.mult,
+                            op1=ALU.mult,
+                            accum_out=sum_er[:, b : b + 1],
+                        )
+                    s = stats.tile([P, BLOCKS], F32)
+                    nc.vector.reciprocal(out=s[:], in_=sum_e[:])
+                    nc.vector.tensor_mul(out=s[:], in0=s[:], in1=sum_er[:])
+
+                    grouped = work.tile([P, HALF, PACK], BF16, align_bytes=64)
+                    for b in range(BLOCKS):
+                        p0 = first + b * P
+                        xT = psum.tile([P, D], BF16, tag="xT")
+                        for j in range(CHUNKS):
+                            nc.tensor.transpose(xT[:, j * P : (j + 1) * P], own[:, j, p0 : p0 + P], ident_bf16[:])
+                        scaled = work.tile([P, D], F32, bufs=3)
+                        nc.scalar.activation(out=scaled[:], in_=xT[:], func=ACT.Copy, scale=s[:, b : b + 1])
+                        back = psum.tile([P, CHUNKS, P], F32, tag="back", bufs=2)
+                        for j in range(CHUNKS):
+                            nc.tensor.transpose(back[:, j, :], scaled[:, j * P : (j + 1) * P], ident_f32[:])
+                        nc.vector.tensor_tensor(
+                            out=grouped[:, b * P : (b + 1) * P, :],
+                            in0=back[:].rearrange("p j w -> p w j"),
+                            in1=u[:, :, b * P : (b + 1) * P].rearrange("p j w -> p w j"),
+                            op=ALU.add,
+                        )
+                    nc.vector.quantize_mx(
+                        out=codes[:, i, :].bitcast(FP8X4),
+                        scales=scales[:, i, :],
+                        in_=grouped[:].rearrange("p w t -> p (w t)"),
+                    )
+
+                for w in range(2):
+                    acc = psum.tile([P, HALF], F32, tag="acc", bufs=2)
+                    for i in range(STREAMS):
+                        w_cols = slice((w * STREAMS + i) * OUT, (w * STREAMS + i + 1) * OUT)
+                        nc.tensor.matmul_mx(
+                            out=acc[:],
+                            lhsT=w_codes[:, w_cols].bitcast(FP8X4),
+                            lhsT_scale=w_scales[:, w_cols],
+                            rhs=codes[:, i, :].bitcast(FP8X4),
+                            rhs_scale=scales[:, i, :],
+                            start=(i == 0),
+                            stop=(i == STREAMS - 1),
+                        )
+                    result = work.tile([P, HALF], F32, bufs=4)
+                    nc.scalar.activation(out=result[:], in_=acc[:], func=ACT.Identity, bias=bias[:, w : w + 1])
+                    nc.sync.dma_start(out=out_views[w][n, :, cols], in_=result[:])

@@ -20,6 +20,8 @@ POS = 1024
 HALF = 512
 BLOCKS = HALF // P
 STREAMS = 2
+UNITS = IMAGES * (POS // HALF) * STREAMS
+TILES = UNITS * BLOCKS
 OUT = 128
 
 FLOPS = 2 * (2 * OUT) * (STREAMS * D) * (IMAGES * POS)
@@ -34,7 +36,7 @@ def tile_fr_pb_t_kernel(tc, x1, x2, FE_x1, FE_x2, g1, g2, p1_w, p1_b, p2_w, p2_b
         const = ctx.enter_context(tc.tile_pool(name="const", bufs=1))
         loads = ctx.enter_context(tc.tile_pool(name="loads", bufs=3))
         work = ctx.enter_context(tc.tile_pool(name="work", bufs=2))
-        stats = ctx.enter_context(tc.tile_pool(name="stats", bufs=4))
+        stats = ctx.enter_context(tc.tile_pool(name="stats", bufs=8))
         psum = ctx.enter_context(tc.psum_pool(name="psum", bufs=1))
 
         ident_f32 = const.tile([P, P], F32)
@@ -73,100 +75,188 @@ def tile_fr_pb_t_kernel(tc, x1, x2, FE_x1, FE_x2, g1, g2, p1_w, p1_b, p2_w, p2_b
             in_=w_grouped[:].rearrange("p w i o t -> p (w i o t)"),
         )
 
-        for n in range(IMAGES):
-            maps = []
+
+        maps, r_of, u_of, grouped_of, codes_of, scales_of, acc_of = {}, {}, {}, {}, {}, {}, {}
+        rT_of, e_of, neg_max_of, sum_e_of, inv_of, s_of, xT_of, scaled_of, back_of = {}, {}, {}, {}, {}, {}, {}, {}, {}
+
+        def place(unit):
+            pair, i = divmod(unit, STREAMS)
+            n, half = divmod(pair, POS // HALF)
+            return n, half * HALF, i
+
+        def load_image(n):
+            maps[n] = []
             for which in range(4):
                 loaded = loads.tile([P, CHUNKS, POS], BF16, tag="map%d" % which)
                 nc.sync.dma_start(out=loaded[:], in_=map_views[which][n])
-                maps.append(loaded)
+                maps[n].append(loaded)
 
-            for half in range(POS // HALF):
-                first = half * HALF
-                cols = slice(first, first + HALF)
-                codes = work.tile([P, STREAMS, HALF], U32, align_bytes=64)
-                scales = work.tile([P, STREAMS, HALF], U8, align_bytes=64)
+        def make_u(unit):
+            n, first, i = place(unit)
+            u = work.tile([P, CHUNKS, HALF], F32, tag="u", bufs=4)
+            for j in range(CHUNKS):
+                nc.gpsimd.tensor_tensor(
+                    out=u[:, j, :],
+                    in0=maps[n][1 - i][:, j, first : first + HALF],
+                    in1=maps[n][2 + i][:, j, first : first + HALF],
+                    op=ALU.add,
+                )
+            u_of[unit] = u
 
+        def make_r(unit):
+            n, first, i = place(unit)
+            r = work.tile([P, CHUNKS, HALF], F32, tag="r", bufs=4)
+            for j in range(CHUNKS):
+                g_col = (i * IMAGES + n) * CHUNKS + j
+                nc.vector.scalar_tensor_tensor(
+                    out=r[:, j, :],
+                    in0=maps[n][i][:, j, first : first + HALF],
+                    scalar=gate[:, g_col : g_col + 1],
+                    in1=maps[n][1 - i][:, j, first : first + HALF],
+                    op0=ALU.mult,
+                    op1=ALU.add,
+                )
+            r_of[unit] = r
+
+        def transpose_r(t):
+            unit, b = divmod(t, BLOCKS)
+            rT = psum.tile([P, D], F32, tag="rT", bufs=3)
+            for j in range(CHUNKS):
+                nc.tensor.transpose(rT[:, j * P : (j + 1) * P], r_of[unit][:, j, b * P : (b + 1) * P], ident_f32[:])
+            rT_of[t] = rT
+
+        def first_exp(t):
+            e = work.tile([P, D], F32, tag="e", bufs=3)
+            nc.scalar.activation(out=e[:], in_=rT_of[t][:], func=ACT.Exp)
+            e_of[t] = e
+
+        def take_max(t):
+            neg_max = stats.tile([P, 1], F32, tag="neg_max")
+            nc.vector.tensor_reduce(out=neg_max[:], in_=e_of[t][:], axis=mybir.AxisListType.X, op=ALU.max, negate=True)
+            neg_max_of[t] = neg_max
+
+        def second_exp(t):
+            sum_e = stats.tile([P, 1], F32, tag="sum_e")
+            nc.scalar.activation(
+                out=e_of[t][:], in_=e_of[t][:], func=ACT.Exp, bias=neg_max_of[t][:], accum_out=sum_e[:]
+            )
+            sum_e_of[t] = sum_e
+
+        def invert_sum(t):
+            inv = stats.tile([P, 1], F32, tag="inv")
+            nc.vector.reciprocal(out=inv[:], in_=sum_e_of[t][:])
+            inv_of[t] = inv
+
+        def weighted_mean(t):
+            s = stats.tile([P, 1], F32, tag="s")
+            nc.vector.scalar_tensor_tensor(
+                out=e_of[t][:],
+                in0=e_of[t][:],
+                scalar=inv_of[t][:],
+                in1=rT_of[t][:],
+                op0=ALU.mult,
+                op1=ALU.mult,
+                accum_out=s[:],
+            )
+            s_of[t] = s
+
+        def transpose_own(t):
+            unit, b = divmod(t, BLOCKS)
+            n, first, i = place(unit)
+            p0 = first + b * P
+            xT = psum.tile([P, D], BF16, tag="xT")
+            for j in range(CHUNKS):
+                nc.tensor.transpose(xT[:, j * P : (j + 1) * P], maps[n][i][:, j, p0 : p0 + P], ident_bf16[:])
+            xT_of[t] = xT
+
+        def scale_own(t):
+            scaled = work.tile([P, D], F32, tag="scaled", bufs=2)
+            nc.scalar.activation(out=scaled[:], in_=xT_of[t][:], func=ACT.Copy, scale=s_of[t][:])
+            scaled_of[t] = scaled
+
+        def transpose_back(t):
+            back = psum.tile([P, CHUNKS, P], F32, tag="back", bufs=2)
+            for j in range(CHUNKS):
+                nc.tensor.transpose(back[:, j, :], scaled_of[t][:, j * P : (j + 1) * P], ident_f32[:])
+            back_of[t] = back
+
+        def add_rest(t):
+            unit, b = divmod(t, BLOCKS)
+            if b == 0:
+                grouped = work.tile([P, HALF, PACK], BF16, tag="grouped", bufs=2, align_bytes=64)
+                grouped_of[unit] = grouped
+            nc.vector.tensor_tensor(
+                out=grouped_of[unit][:, b * P : (b + 1) * P, :],
+                in0=back_of[t][:].rearrange("p j w -> p w j"),
+                in1=u_of[unit][:, :, b * P : (b + 1) * P].rearrange("p j w -> p w j"),
+                op=ALU.add,
+            )
+
+        def quantise(unit):
+            pair, i = divmod(unit, STREAMS)
+            if i == 0:
+                codes = work.tile([P, STREAMS, HALF], U32, tag="codes", bufs=2, align_bytes=64)
+                scales = work.tile([P, STREAMS, HALF], U8, tag="scales", bufs=2, align_bytes=64)
+                codes_of[pair], scales_of[pair] = codes, scales
+            nc.vector.quantize_mx(
+                out=codes_of[pair][:, i, :].bitcast(FP8X4),
+                scales=scales_of[pair][:, i, :],
+                in_=grouped_of[unit][:].rearrange("p w t -> p (w t)"),
+            )
+
+        def project(pair):
+            for w in range(2):
+                acc = psum.tile([P, HALF], F32, tag="acc", bufs=2)
                 for i in range(STREAMS):
-                    own, other, extra = maps[i], maps[1 - i], maps[2 + i]
-
-                    r = work.tile([P, CHUNKS, HALF], F32)
-                    for j in range(CHUNKS):
-                        g_col = (i * IMAGES + n) * CHUNKS + j
-                        nc.vector.scalar_tensor_tensor(
-                            out=r[:, j, :],
-                            in0=own[:, j, cols],
-                            scalar=gate[:, g_col : g_col + 1],
-                            in1=other[:, j, cols],
-                            op0=ALU.mult,
-                            op1=ALU.add,
-                        )
-                    u = work.tile([P, CHUNKS, HALF], F32)
-                    nc.gpsimd.tensor_tensor(out=u[:], in0=other[:, :, cols], in1=extra[:, :, cols], op=ALU.add)
-
-                    sum_e = stats.tile([P, BLOCKS], F32)
-                    sum_er = stats.tile([P, BLOCKS], F32)
-                    for b in range(BLOCKS):
-                        rT = psum.tile([P, D], F32, tag="rT", bufs=3)
-                        for j in range(CHUNKS):
-                            nc.tensor.transpose(rT[:, j * P : (j + 1) * P], r[:, j, b * P : (b + 1) * P], ident_f32[:])
-                        e = work.tile([P, D], F32, bufs=4)
-                        nc.scalar.activation(out=e[:], in_=rT[:], func=ACT.Exp)
-                        neg_max = stats.tile([P, 1], F32)
-                        nc.vector.tensor_reduce(
-                            out=neg_max[:], in_=e[:], axis=mybir.AxisListType.X, op=ALU.max, negate=True
-                        )
-                        nc.scalar.activation(
-                            out=e[:], in_=e[:], func=ACT.Exp, bias=neg_max[:], accum_out=sum_e[:, b : b + 1]
-                        )
-                        nc.vector.scalar_tensor_tensor(
-                            out=e[:],
-                            in0=e[:],
-                            scalar=1.0,
-                            in1=rT[:],
-                            op0=ALU.mult,
-                            op1=ALU.mult,
-                            accum_out=sum_er[:, b : b + 1],
-                        )
-                    s = stats.tile([P, BLOCKS], F32)
-                    nc.vector.reciprocal(out=s[:], in_=sum_e[:])
-                    nc.vector.tensor_mul(out=s[:], in0=s[:], in1=sum_er[:])
-
-                    grouped = work.tile([P, HALF, PACK], BF16, align_bytes=64)
-                    for b in range(BLOCKS):
-                        p0 = first + b * P
-                        xT = psum.tile([P, D], BF16, tag="xT")
-                        for j in range(CHUNKS):
-                            nc.tensor.transpose(xT[:, j * P : (j + 1) * P], own[:, j, p0 : p0 + P], ident_bf16[:])
-                        scaled = work.tile([P, D], F32, bufs=3)
-                        nc.scalar.activation(out=scaled[:], in_=xT[:], func=ACT.Copy, scale=s[:, b : b + 1])
-                        back = psum.tile([P, CHUNKS, P], F32, tag="back", bufs=2)
-                        for j in range(CHUNKS):
-                            nc.tensor.transpose(back[:, j, :], scaled[:, j * P : (j + 1) * P], ident_f32[:])
-                        nc.vector.tensor_tensor(
-                            out=grouped[:, b * P : (b + 1) * P, :],
-                            in0=back[:].rearrange("p j w -> p w j"),
-                            in1=u[:, :, b * P : (b + 1) * P].rearrange("p j w -> p w j"),
-                            op=ALU.add,
-                        )
-                    nc.vector.quantize_mx(
-                        out=codes[:, i, :].bitcast(FP8X4),
-                        scales=scales[:, i, :],
-                        in_=grouped[:].rearrange("p w t -> p (w t)"),
+                    w_cols = slice((w * STREAMS + i) * OUT, (w * STREAMS + i + 1) * OUT)
+                    nc.tensor.matmul_mx(
+                        out=acc[:],
+                        lhsT=w_codes[:, w_cols].bitcast(FP8X4),
+                        lhsT_scale=w_scales[:, w_cols],
+                        rhs=codes_of[pair][:, i, :].bitcast(FP8X4),
+                        rhs_scale=scales_of[pair][:, i, :],
+                        start=(i == 0),
+                        stop=(i == STREAMS - 1),
                     )
+                acc_of[(pair, w)] = acc
 
-                for w in range(2):
-                    acc = psum.tile([P, HALF], F32, tag="acc", bufs=2)
-                    for i in range(STREAMS):
-                        w_cols = slice((w * STREAMS + i) * OUT, (w * STREAMS + i + 1) * OUT)
-                        nc.tensor.matmul_mx(
-                            out=acc[:],
-                            lhsT=w_codes[:, w_cols].bitcast(FP8X4),
-                            lhsT_scale=w_scales[:, w_cols],
-                            rhs=codes[:, i, :].bitcast(FP8X4),
-                            rhs_scale=scales[:, i, :],
-                            start=(i == 0),
-                            stop=(i == STREAMS - 1),
-                        )
-                    result = work.tile([P, HALF], F32, bufs=4)
-                    nc.scalar.activation(out=result[:], in_=acc[:], func=ACT.Identity, bias=bias[:, w : w + 1])
-                    nc.sync.dma_start(out=out_views[w][n, :, cols], in_=result[:])
+        def store(pair):
+            n, first = place(pair * STREAMS)[:2]
+            for w in range(2):
+                result = work.tile([P, HALF], F32, tag="result", bufs=4)
+                nc.scalar.activation(out=result[:], in_=acc_of[(pair, w)][:], func=ACT.Identity, bias=bias[:, w : w + 1])
+                nc.sync.dma_start(out=out_views[w][n, :, first : first + HALF], in_=result[:])
+
+        with tc.manual_schedule():
+            for step in range(-16, TILES + 6):
+                if step % 16 == 0 and step // 16 + 1 < IMAGES:
+                    load_image(step // 16 + 1)
+                if step % BLOCKS == 0 and 0 <= step // BLOCKS + 2 < UNITS:
+                    make_u(step // BLOCKS + 2)
+
+                if 0 <= step + 1 < TILES:
+                    transpose_r(step + 1)
+                if 0 <= step < TILES:
+                    first_exp(step)
+                    take_max(step)
+                if step % BLOCKS == 0 and 0 <= step // BLOCKS - 2 < UNITS:
+                    quantise(step // BLOCKS - 2)
+                if 0 <= step - 1 < TILES:
+                    second_exp(step - 1)
+                    invert_sum(step - 1)
+                if 0 <= step - 3 < TILES:
+                    scale_own(step - 3)
+                    transpose_back(step - 3)
+                if 0 <= step - 2 < TILES:
+                    transpose_own(step - 2)
+                if 0 <= step - 4 < TILES:
+                    add_rest(step - 4)
+                if 0 <= step - 1 < TILES:
+                    weighted_mean(step - 1)
+                if step % 8 == 3 and 0 <= step // 8 + 1 < UNITS // STREAMS:
+                    make_r((step // 8 + 1) * STREAMS)
+                    make_r((step // 8 + 1) * STREAMS + 1)
+                if step % 8 == 4 and 0 <= step // 8 - 1:
+                    project(step // 8 - 1)
+                if step % 8 == 5 and 0 <= step // 8 - 1:
+                    store(step // 8 - 1)

@@ -19,6 +19,7 @@ CHUNKS = D // P
 POS = 1024
 HALF = 512
 BLOCKS = HALF // P
+QUARTER = 256
 STREAMS = 2
 UNITS = IMAGES * (POS // HALF) * STREAMS
 TILES = UNITS * BLOCKS
@@ -50,7 +51,7 @@ def tile_fr_pb_t_kernel(tc, x1, x2, FE_x1, FE_x2, g1, g2, p1_w, p1_b, p2_w, p2_b
         nc.sync.dma_start(out=rows[24:48, :], in_=g2.rearrange("n (j p) -> (n j) p", p=P))
         nc.sync.dma_start(out=rows[48:49, :], in_=p1_b.rearrange("(o p) -> o p", o=1))
         nc.sync.dma_start(out=rows[49:50, :], in_=p2_b.rearrange("(o p) -> o p", o=1))
-        columns = psum.tile([P, P], BF16, tag="xT")
+        columns = psum.tile([P, P], BF16, tag="xT", bufs=2)
         nc.tensor.transpose(columns[:], rows[:], ident_bf16[:])
         gate = const.tile([P, STREAMS * IMAGES * CHUNKS], F32)
         nc.scalar.activation(out=gate[:], in_=columns[:, 0:48], func=ACT.Sigmoid)
@@ -61,7 +62,7 @@ def tile_fr_pb_t_kernel(tc, x1, x2, FE_x1, FE_x2, g1, g2, p1_w, p1_b, p2_w, p2_b
         for w, weight in enumerate((p1_w, p2_w)):
             w_raw = const.tile([P, STREAMS * D], BF16, tag="w_raw%d" % w)
             nc.sync.dma_start(out=w_raw[:], in_=weight)
-            wT = psum.tile([P, STREAMS, PACK, OUT], BF16, tag="xT")
+            wT = psum.tile([P, STREAMS, PACK, OUT], BF16, tag="xT", bufs=2)
             for i in range(STREAMS):
                 for t in range(PACK):
                     k0 = D * i + P * t
@@ -76,7 +77,7 @@ def tile_fr_pb_t_kernel(tc, x1, x2, FE_x1, FE_x2, g1, g2, p1_w, p1_b, p2_w, p2_b
         )
 
 
-        maps, r_of, u_of, grouped_of, codes_of, scales_of, acc_of = {}, {}, {}, {}, {}, {}, {}
+        maps, r_of, u_of, grouped_of, codes_of, scales_of, acc_of, result_of = {}, {}, {}, {}, {}, {}, {}, {}
         rT_of, e_of, neg_max_of, sum_e_of, inv_of, s_of, xT_of, scaled_of, back_of = {}, {}, {}, {}, {}, {}, {}, {}, {}
 
         def place(unit):
@@ -164,7 +165,7 @@ def tile_fr_pb_t_kernel(tc, x1, x2, FE_x1, FE_x2, g1, g2, p1_w, p1_b, p2_w, p2_b
             unit, b = divmod(t, BLOCKS)
             n, first, i = place(unit)
             p0 = first + b * P
-            xT = psum.tile([P, D], BF16, tag="xT")
+            xT = psum.tile([P, D], BF16, tag="xT", bufs=2)
             for j in range(CHUNKS):
                 nc.tensor.transpose(xT[:, j * P : (j + 1) * P], maps[n][i][:, j, p0 : p0 + P], ident_bf16[:])
             xT_of[t] = xT
@@ -204,36 +205,49 @@ def tile_fr_pb_t_kernel(tc, x1, x2, FE_x1, FE_x2, g1, g2, p1_w, p1_b, p2_w, p2_b
                 in_=grouped_of[unit][:].rearrange("p w t -> p (w t)"),
             )
 
-        def project(pair):
+        def project(pair, quarter):
+            acc = psum.tile([P, 2, QUARTER], F32, tag="acc")
+            q_cols = slice(quarter * QUARTER, (quarter + 1) * QUARTER)
             for w in range(2):
-                acc = psum.tile([P, HALF], F32, tag="acc", bufs=2)
                 for i in range(STREAMS):
                     w_cols = slice((w * STREAMS + i) * OUT, (w * STREAMS + i + 1) * OUT)
                     nc.tensor.matmul_mx(
-                        out=acc[:],
+                        out=acc[:, w, :],
                         lhsT=w_codes[:, w_cols].bitcast(FP8X4),
                         lhsT_scale=w_scales[:, w_cols],
-                        rhs=codes_of[pair][:, i, :].bitcast(FP8X4),
-                        rhs_scale=scales_of[pair][:, i, :],
+                        rhs=codes_of[pair][:, i, q_cols].bitcast(FP8X4),
+                        rhs_scale=scales_of[pair][:, i, q_cols],
                         start=(i == 0),
                         stop=(i == STREAMS - 1),
                     )
-                acc_of[(pair, w)] = acc
+            acc_of[(pair, quarter)] = acc
 
-        def store(pair):
+        def store(pair, quarter):
             n, first = place(pair * STREAMS)[:2]
+            if quarter == 0:
+                result = work.tile([P, 2, HALF], F32, tag="result", bufs=2)
+                result_of[pair] = result
+            q_cols = slice(quarter * QUARTER, (quarter + 1) * QUARTER)
             for w in range(2):
-                result = work.tile([P, HALF], F32, tag="result", bufs=4)
-                nc.scalar.activation(out=result[:], in_=acc_of[(pair, w)][:], func=ACT.Identity, bias=bias[:, w : w + 1])
-                nc.sync.dma_start(out=out_views[w][n, :, first : first + HALF], in_=result[:])
+                nc.scalar.activation(
+                    out=result_of[pair][:, w, q_cols],
+                    in_=acc_of[(pair, quarter)][:, w, :],
+                    func=ACT.Identity,
+                    bias=bias[:, w : w + 1],
+                )
+            if quarter == 1:
+                for w in range(2):
+                    nc.sync.dma_start(out=out_views[w][n, :, first : first + HALF], in_=result_of[pair][:, w, :])
 
         with tc.manual_schedule():
-            for step in range(-16, TILES + 6):
+            for step in range(-16, TILES + 8):
                 if step % 16 == 0 and step // 16 + 1 < IMAGES:
                     load_image(step // 16 + 1)
                 if step % BLOCKS == 0 and 0 <= step // BLOCKS + 2 < UNITS:
                     make_u(step // BLOCKS + 2)
 
+                if 0 <= step - 2 < TILES:
+                    transpose_own(step - 2)
                 if 0 <= step + 1 < TILES:
                     transpose_r(step + 1)
                 if 0 <= step < TILES:
@@ -247,8 +261,6 @@ def tile_fr_pb_t_kernel(tc, x1, x2, FE_x1, FE_x2, g1, g2, p1_w, p1_b, p2_w, p2_b
                 if 0 <= step - 3 < TILES:
                     scale_own(step - 3)
                     transpose_back(step - 3)
-                if 0 <= step - 2 < TILES:
-                    transpose_own(step - 2)
                 if 0 <= step - 4 < TILES:
                     add_rest(step - 4)
                 if 0 <= step - 1 < TILES:
@@ -256,7 +268,11 @@ def tile_fr_pb_t_kernel(tc, x1, x2, FE_x1, FE_x2, g1, g2, p1_w, p1_b, p2_w, p2_b
                 if step % 8 == 3 and 0 <= step // 8 + 1 < UNITS // STREAMS:
                     make_r((step // 8 + 1) * STREAMS)
                     make_r((step // 8 + 1) * STREAMS + 1)
-                if step % 8 == 4 and 0 <= step // 8 - 1:
-                    project(step // 8 - 1)
-                if step % 8 == 5 and 0 <= step // 8 - 1:
-                    store(step // 8 - 1)
+                if step >= 12 and step % 8 == 4:
+                    project(step // 8 - 1, 0)
+                if step >= 12 and step % 8 == 5:
+                    store(step // 8 - 1, 0)
+                if step >= 12 and step % 8 == 6:
+                    project(step // 8 - 1, 1)
+                if step >= 12 and step % 8 == 7:
+                    store(step // 8 - 1, 1)

@@ -21,7 +21,8 @@ HALF = 512
 BLOCKS = HALF // P
 QUARTER = 256
 STREAMS = 2
-UNITS = IMAGES * (POS // HALF) * STREAMS
+PAIRS = IMAGES * (POS // HALF)
+UNITS = PAIRS * STREAMS
 TILES = UNITS * BLOCKS
 OUT = 128
 
@@ -35,7 +36,7 @@ def tile_fr_pb_t_kernel(tc, x1, x2, FE_x1, FE_x2, g1, g2, p1_w, p1_b, p2_w, p2_b
 
     with ExitStack() as ctx:
         const = ctx.enter_context(tc.tile_pool(name="const", bufs=1))
-        loads = ctx.enter_context(tc.tile_pool(name="loads", bufs=3))
+        loads = ctx.enter_context(tc.tile_pool(name="loads", bufs=4))
         work = ctx.enter_context(tc.tile_pool(name="work", bufs=2))
         stats = ctx.enter_context(tc.tile_pool(name="stats", bufs=8))
         psum = ctx.enter_context(tc.psum_pool(name="psum", bufs=1))
@@ -80,40 +81,32 @@ def tile_fr_pb_t_kernel(tc, x1, x2, FE_x1, FE_x2, g1, g2, p1_w, p1_b, p2_w, p2_b
         maps, r_of, u_of, grouped_of, codes_of, scales_of, acc_of, result_of = {}, {}, {}, {}, {}, {}, {}, {}
         rT_of, e_of, neg_max_of, sum_e_of, inv_of, s_of, xT_of, scaled_of, back_of = {}, {}, {}, {}, {}, {}, {}, {}, {}
 
-        def place(unit):
-            pair, i = divmod(unit, STREAMS)
+        def load_pair(pair):
             n, half = divmod(pair, POS // HALF)
-            return n, half * HALF, i
-
-        def load_image(n):
-            maps[n] = []
+            maps[pair] = []
             for which in range(4):
-                loaded = loads.tile([P, CHUNKS, POS], BF16, tag="map%d" % which)
-                nc.sync.dma_start(out=loaded[:], in_=map_views[which][n])
-                maps[n].append(loaded)
+                loaded = loads.tile([P, CHUNKS, HALF], BF16, tag="map%d" % which)
+                nc.sync.dma_start(out=loaded[:], in_=map_views[which][n][:, :, half * HALF : (half + 1) * HALF])
+                maps[pair].append(loaded)
 
         def make_u(unit):
-            n, first, i = place(unit)
+            pair, i = divmod(unit, STREAMS)
             u = work.tile([P, CHUNKS, HALF], F32, tag="u", bufs=4)
             for j in range(CHUNKS):
-                nc.gpsimd.tensor_tensor(
-                    out=u[:, j, :],
-                    in0=maps[n][1 - i][:, j, first : first + HALF],
-                    in1=maps[n][2 + i][:, j, first : first + HALF],
-                    op=ALU.add,
-                )
+                nc.gpsimd.tensor_tensor(out=u[:, j, :], in0=maps[pair][1 - i][:, j, :], in1=maps[pair][2 + i][:, j, :], op=ALU.add)
             u_of[unit] = u
 
         def make_r(unit):
-            n, first, i = place(unit)
-            r = work.tile([P, CHUNKS, HALF], F32, tag="r", bufs=4)
+            pair, i = divmod(unit, STREAMS)
+            n = pair // (POS // HALF)
+            r = work.tile([P, CHUNKS, HALF], F32, tag="r", bufs=3)
             for j in range(CHUNKS):
                 g_col = (i * IMAGES + n) * CHUNKS + j
                 nc.vector.scalar_tensor_tensor(
                     out=r[:, j, :],
-                    in0=maps[n][i][:, j, first : first + HALF],
+                    in0=maps[pair][i][:, j, :],
                     scalar=gate[:, g_col : g_col + 1],
-                    in1=maps[n][1 - i][:, j, first : first + HALF],
+                    in1=maps[pair][1 - i][:, j, :],
                     op0=ALU.mult,
                     op1=ALU.add,
                 )
@@ -121,7 +114,7 @@ def tile_fr_pb_t_kernel(tc, x1, x2, FE_x1, FE_x2, g1, g2, p1_w, p1_b, p2_w, p2_b
 
         def transpose_r(t):
             unit, b = divmod(t, BLOCKS)
-            rT = psum.tile([P, D], F32, tag="rT", bufs=3)
+            rT = psum.tile([P, D], F32, tag="rT", bufs=4)
             for j in range(CHUNKS):
                 nc.tensor.transpose(rT[:, j * P : (j + 1) * P], r_of[unit][:, j, b * P : (b + 1) * P], ident_f32[:])
             rT_of[t] = rT
@@ -163,11 +156,10 @@ def tile_fr_pb_t_kernel(tc, x1, x2, FE_x1, FE_x2, g1, g2, p1_w, p1_b, p2_w, p2_b
 
         def transpose_own(t):
             unit, b = divmod(t, BLOCKS)
-            n, first, i = place(unit)
-            p0 = first + b * P
+            pair, i = divmod(unit, STREAMS)
             xT = psum.tile([P, D], BF16, tag="xT", bufs=2)
             for j in range(CHUNKS):
-                nc.tensor.transpose(xT[:, j * P : (j + 1) * P], maps[n][i][:, j, p0 : p0 + P], ident_bf16[:])
+                nc.tensor.transpose(xT[:, j * P : (j + 1) * P], maps[pair][i][:, j, b * P : (b + 1) * P], ident_bf16[:])
             xT_of[t] = xT
 
         def scale_own(t):
@@ -206,7 +198,7 @@ def tile_fr_pb_t_kernel(tc, x1, x2, FE_x1, FE_x2, g1, g2, p1_w, p1_b, p2_w, p2_b
             )
 
         def project(pair, quarter):
-            acc = psum.tile([P, 2, QUARTER], F32, tag="acc")
+            acc = psum.tile([P, 2, QUARTER], F32, tag="rT", bufs=4)
             q_cols = slice(quarter * QUARTER, (quarter + 1) * QUARTER)
             for w in range(2):
                 for i in range(STREAMS):
@@ -223,7 +215,7 @@ def tile_fr_pb_t_kernel(tc, x1, x2, FE_x1, FE_x2, g1, g2, p1_w, p1_b, p2_w, p2_b
             acc_of[(pair, quarter)] = acc
 
         def store(pair, quarter):
-            n, first = place(pair * STREAMS)[:2]
+            n, half = divmod(pair, POS // HALF)
             if quarter == 0:
                 result = work.tile([P, 2, HALF], F32, tag="result", bufs=2)
                 result_of[pair] = result
@@ -237,19 +229,19 @@ def tile_fr_pb_t_kernel(tc, x1, x2, FE_x1, FE_x2, g1, g2, p1_w, p1_b, p2_w, p2_b
                 )
             if quarter == 1:
                 for w in range(2):
-                    nc.sync.dma_start(out=out_views[w][n, :, first : first + HALF], in_=result_of[pair][:, w, :])
+                    nc.sync.dma_start(out=out_views[w][n, :, half * HALF : (half + 1) * HALF], in_=result_of[pair][:, w, :])
 
         with tc.manual_schedule():
             for step in range(-16, TILES + 8):
-                if step % 16 == 0 and step // 16 + 1 < IMAGES:
-                    load_image(step // 16 + 1)
+                if step % 8 == 0 and step // 8 + 2 < PAIRS:
+                    load_pair(step // 8 + 2)
                 if step % BLOCKS == 0 and 0 <= step // BLOCKS + 2 < UNITS:
                     make_u(step // BLOCKS + 2)
 
-                if 0 <= step - 2 < TILES:
-                    transpose_own(step - 2)
                 if 0 <= step + 1 < TILES:
                     transpose_r(step + 1)
+                if 0 <= step - 2 < TILES:
+                    transpose_own(step - 2)
                 if 0 <= step < TILES:
                     first_exp(step)
                     take_max(step)
@@ -265,8 +257,9 @@ def tile_fr_pb_t_kernel(tc, x1, x2, FE_x1, FE_x2, g1, g2, p1_w, p1_b, p2_w, p2_b
                     add_rest(step - 4)
                 if 0 <= step - 1 < TILES:
                     weighted_mean(step - 1)
-                if step % 8 == 3 and 0 <= step // 8 + 1 < UNITS // STREAMS:
+                if step % 8 == 5 and 0 <= step // 8 + 1 < PAIRS:
                     make_r((step // 8 + 1) * STREAMS)
+                if step % 8 == 7 and 0 <= step // 8 + 1 < PAIRS:
                     make_r((step // 8 + 1) * STREAMS + 1)
                 if step >= 12 and step % 8 == 4:
                     project(step // 8 - 1, 0)

@@ -24,6 +24,9 @@ STREAMS = 2
 PAIRS = IMAGES * (POS // HALF)
 UNITS = PAIRS * STREAMS
 TILES = UNITS * BLOCKS
+LOAD_LEAD = 20
+R_LEAD = 12
+U_LEAD = 8
 OUT = 128
 
 FLOPS = 2 * (2 * OUT) * (STREAMS * D) * (IMAGES * POS)
@@ -89,28 +92,53 @@ def tile_fr_pb_t_kernel(tc, x1, x2, FE_x1, FE_x2, g1, g2, p1_w, p1_b, p2_w, p2_b
                 nc.sync.dma_start(out=loaded[:], in_=map_views[which][n][:, :, half * HALF : (half + 1) * HALF])
                 maps[pair].append(loaded)
 
-        def make_u(unit):
+        def gate_column(unit, j):
             pair, i = divmod(unit, STREAMS)
-            u = work.tile([P, CHUNKS, HALF], F32, tag="u", bufs=4)
-            for j in range(CHUNKS):
-                nc.gpsimd.tensor_tensor(out=u[:, j, :], in0=maps[pair][1 - i][:, j, :], in1=maps[pair][2 + i][:, j, :], op=ALU.add)
-            u_of[unit] = u
+            g_col = (i * IMAGES + pair // (POS // HALF)) * CHUNKS + j
+            return gate[:, g_col : g_col + 1]
 
-        def make_r(unit):
+        def make_u(unit, j):
             pair, i = divmod(unit, STREAMS)
-            n = pair // (POS // HALF)
-            r = work.tile([P, CHUNKS, HALF], F32, tag="r", bufs=3)
+            if j == 0:
+                u = work.tile([P, CHUNKS, HALF], F32, tag="u", bufs=4)
+                u_of[unit] = u
+            nc.gpsimd.tensor_tensor(
+                out=u_of[unit][:, j, :], in0=maps[pair][1 - i][:, j, :], in1=maps[pair][2 + i][:, j, :], op=ALU.add
+            )
+
+        def make_r_on_vector(unit):
+            pair, i = divmod(unit, STREAMS)
+            r = work.tile([P, CHUNKS, HALF], F32, tag="r_vector", bufs=2)
             for j in range(CHUNKS):
-                g_col = (i * IMAGES + n) * CHUNKS + j
                 nc.vector.scalar_tensor_tensor(
                     out=r[:, j, :],
                     in0=maps[pair][i][:, j, :],
-                    scalar=gate[:, g_col : g_col + 1],
+                    scalar=gate_column(unit, j),
                     in1=maps[pair][1 - i][:, j, :],
                     op0=ALU.mult,
                     op1=ALU.add,
                 )
             r_of[unit] = r
+
+        def make_r_on_gpsimd(unit, piece):
+            pair, i = divmod(unit, STREAMS)
+            if piece == 0:
+                r = work.tile([P, CHUNKS, HALF], F32, tag="r_gpsimd", bufs=3)
+                r_of[unit] = r
+            j = piece % CHUNKS
+            if piece < CHUNKS:
+                nc.gpsimd.tensor_scalar(
+                    out=r_of[unit][:, j, :],
+                    in0=maps[pair][i][:, j, :],
+                    scalar1=gate_column(unit, j),
+                    scalar2=0.0,
+                    op0=ALU.mult,
+                    op1=ALU.add,
+                )
+            else:
+                nc.gpsimd.tensor_tensor(
+                    out=r_of[unit][:, j, :], in0=r_of[unit][:, j, :], in1=maps[pair][1 - i][:, j, :], op=ALU.add
+                )
 
         def transpose_r(t):
             unit, b = divmod(t, BLOCKS)
@@ -232,11 +260,13 @@ def tile_fr_pb_t_kernel(tc, x1, x2, FE_x1, FE_x2, g1, g2, p1_w, p1_b, p2_w, p2_b
                     nc.sync.dma_start(out=out_views[w][n, :, half * HALF : (half + 1) * HALF], in_=result_of[pair][:, w, :])
 
         with tc.manual_schedule():
-            for step in range(-16, TILES + 8):
-                if step % 8 == 0 and step // 8 + 2 < PAIRS:
-                    load_pair(step // 8 + 2)
-                if step % BLOCKS == 0 and 0 <= step // BLOCKS + 2 < UNITS:
-                    make_u(step // BLOCKS + 2)
+            for step in range(-LOAD_LEAD, TILES + 8):
+                if (step + LOAD_LEAD) % 8 == 0 and (step + LOAD_LEAD) // 8 < PAIRS:
+                    load_pair((step + LOAD_LEAD) // 8)
+                if 0 <= step + R_LEAD < TILES:
+                    make_r_on_gpsimd((step + R_LEAD) // 8 * STREAMS + 1, (step + R_LEAD) % 8)
+                if 0 <= step + U_LEAD < TILES:
+                    make_u((step + U_LEAD) // BLOCKS, (step + U_LEAD) % BLOCKS)
 
                 if 0 <= step + 1 < TILES:
                     transpose_r(step + 1)
@@ -258,9 +288,7 @@ def tile_fr_pb_t_kernel(tc, x1, x2, FE_x1, FE_x2, g1, g2, p1_w, p1_b, p2_w, p2_b
                 if 0 <= step - 1 < TILES:
                     weighted_mean(step - 1)
                 if step % 8 == 5 and 0 <= step // 8 + 1 < PAIRS:
-                    make_r((step // 8 + 1) * STREAMS)
-                if step % 8 == 7 and 0 <= step // 8 + 1 < PAIRS:
-                    make_r((step // 8 + 1) * STREAMS + 1)
+                    make_r_on_vector((step // 8 + 1) * STREAMS)
                 if step >= 12 and step % 8 == 4:
                     project(step // 8 - 1, 0)
                 if step >= 12 and step % 8 == 5:

@@ -120,20 +120,15 @@ def tile_fr_pb_t_kernel(tc, x1, x2, FE_x1, FE_x2, g1, g2, p1_w, p1_b, p2_w, p2_b
                 )
             r_of[unit] = r
 
-        def make_r_on_gpsimd(unit, piece):
+        def make_r_in_pieces(unit, piece):
             pair, i = divmod(unit, STREAMS)
             if piece == 0:
-                r = work.tile([P, CHUNKS, HALF], F32, tag="r_gpsimd", bufs=3)
+                r = work.tile([P, CHUNKS, HALF], F32, tag="r_pieces", bufs=3)
                 r_of[unit] = r
             j = piece % CHUNKS
             if piece < CHUNKS:
-                nc.gpsimd.tensor_scalar(
-                    out=r_of[unit][:, j, :],
-                    in0=maps[pair][i][:, j, :],
-                    scalar1=gate_column(unit, j),
-                    scalar2=0.0,
-                    op0=ALU.mult,
-                    op1=ALU.add,
+                nc.scalar.activation(
+                    out=r_of[unit][:, j, :], in_=maps[pair][i][:, j, :], func=ACT.Copy, scale=gate_column(unit, j)
                 )
             else:
                 nc.gpsimd.tensor_tensor(
@@ -264,7 +259,7 @@ def tile_fr_pb_t_kernel(tc, x1, x2, FE_x1, FE_x2, g1, g2, p1_w, p1_b, p2_w, p2_b
                 if (step + LOAD_LEAD) % 8 == 0 and (step + LOAD_LEAD) // 8 < PAIRS:
                     load_pair((step + LOAD_LEAD) // 8)
                 if 0 <= step + R_LEAD < TILES:
-                    make_r_on_gpsimd((step + R_LEAD) // 8 * STREAMS + 1, (step + R_LEAD) % 8)
+                    make_r_in_pieces((step + R_LEAD) // 8 * STREAMS + 1, (step + R_LEAD) % 8)
                 if 0 <= step + U_LEAD < TILES:
                     make_u((step + U_LEAD) // BLOCKS, (step + U_LEAD) % BLOCKS)
 

from contextlib import ExitStack

import concourse.mybir as mybir
from concourse.masks import make_identity

F32 = mybir.dt.float32
BF16 = mybir.dt.bfloat16
U32 = mybir.dt.uint32
U8 = mybir.dt.uint8
FP8X4 = mybir.dt.float8_e4m3fn_x4
ALU = mybir.AluOpType
ACT = mybir.ActivationFunctionType

P = 128
PACK = 4
IMAGES = 6
D = 512
CHUNKS = D // P
POS = 1024
HALF = 512
BLOCKS = HALF // P
QUARTER = 256
STREAMS = 2
PAIRS = IMAGES * (POS // HALF)
UNITS = PAIRS * STREAMS
TILES = UNITS * BLOCKS
LOAD_LEAD = 20
R_LEAD = 12
U_LEAD = 8
OUT = 128

FLOPS = 2 * (2 * OUT) * (STREAMS * D) * (IMAGES * POS)


def tile_fr_pb_t_kernel(tc, x1, x2, FE_x1, FE_x2, g1, g2, p1_w, p1_b, p2_w, p2_b, out_0, out_1):
    nc = tc.nc
    map_views = [m.rearrange("n (j p) h w -> n p j (h w)", p=P) for m in (x1, x2, FE_x1, FE_x2)]
    out_views = [o.rearrange("n o h w -> n o (h w)") for o in (out_0, out_1)]

    with ExitStack() as ctx:
        const = ctx.enter_context(tc.tile_pool(name="const", bufs=1))
        loads = ctx.enter_context(tc.tile_pool(name="loads", bufs=4))
        work = ctx.enter_context(tc.tile_pool(name="work", bufs=2))
        stats = ctx.enter_context(tc.tile_pool(name="stats", bufs=8))
        psum = ctx.enter_context(tc.psum_pool(name="psum", bufs=1))

        ident_f32 = const.tile([P, P], F32)
        make_identity(nc, ident_f32[:])
        ident_bf16 = const.tile([P, P], BF16)
        make_identity(nc, ident_bf16[:])

        rows = const.tile([P, P], BF16)
        nc.vector.memset(rows[:], 0.0)
        nc.sync.dma_start(out=rows[0:24, :], in_=g1.rearrange("n (j p) -> (n j) p", p=P))
        nc.sync.dma_start(out=rows[24:48, :], in_=g2.rearrange("n (j p) -> (n j) p", p=P))
        nc.sync.dma_start(out=rows[48:49, :], in_=p1_b.rearrange("(o p) -> o p", o=1))
        nc.sync.dma_start(out=rows[49:50, :], in_=p2_b.rearrange("(o p) -> o p", o=1))
        columns = psum.tile([P, P], BF16, tag="xT", bufs=2)
        nc.tensor.transpose(columns[:], rows[:], ident_bf16[:])
        gate = const.tile([P, STREAMS * IMAGES * CHUNKS], F32)
        nc.scalar.activation(out=gate[:], in_=columns[:, 0:48], func=ACT.Sigmoid)
        bias = const.tile([P, 2], F32)
        nc.vector.tensor_copy(out=bias[:], in_=columns[:, 48:50])

        w_grouped = const.tile([P, 2, STREAMS, OUT, PACK], BF16, align_bytes=64)
        for w, weight in enumerate((p1_w, p2_w)):
            w_raw = const.tile([P, STREAMS * D], BF16, tag="w_raw%d" % w)
            nc.sync.dma_start(out=w_raw[:], in_=weight)
            wT = psum.tile([P, STREAMS, PACK, OUT], BF16, tag="xT", bufs=2)
            for i in range(STREAMS):
                for t in range(PACK):
                    k0 = D * i + P * t
                    nc.tensor.transpose(wT[:, i, t, :], w_raw[:, k0 : k0 + P], ident_bf16[:])
            nc.vector.tensor_copy(out=w_grouped[:, w], in_=wT[:].rearrange("p i t o -> p i o t"))
        w_codes = const.tile([P, 2 * STREAMS * OUT], U32, align_bytes=64)
        w_scales = const.tile([P, 2 * STREAMS * OUT], U8, align_bytes=64)
        nc.vector.quantize_mx(
            out=w_codes[:].bitcast(FP8X4),
            scales=w_scales[:],
            in_=w_grouped[:].rearrange("p w i o t -> p (w i o t)"),
        )


        maps, r_of, u_of, grouped_of, codes_of, scales_of, acc_of, result_of = {}, {}, {}, {}, {}, {}, {}, {}
        rT_of, e_of, neg_max_of, sum_e_of, inv_of, s_of, xT_of, scaled_of, back_of = {}, {}, {}, {}, {}, {}, {}, {}, {}

        def load_pair(pair):
            n, half = divmod(pair, POS // HALF)
            maps[pair] = []
            for which in range(4):
                loaded = loads.tile([P, CHUNKS, HALF], BF16, tag="map%d" % which)
                nc.sync.dma_start(out=loaded[:], in_=map_views[which][n][:, :, half * HALF : (half + 1) * HALF])
                maps[pair].append(loaded)

        def gate_column(unit, j):
            pair, i = divmod(unit, STREAMS)
            g_col = (i * IMAGES + pair // (POS // HALF)) * CHUNKS + j
            return gate[:, g_col : g_col + 1]

        def make_u(unit, j):
            pair, i = divmod(unit, STREAMS)
            if j == 0:
                u = work.tile([P, CHUNKS, HALF], F32, tag="u", bufs=4)
                u_of[unit] = u
            nc.gpsimd.tensor_tensor(
                out=u_of[unit][:, j, :], in0=maps[pair][1 - i][:, j, :], in1=maps[pair][2 + i][:, j, :], op=ALU.add
            )

        def make_r_on_vector(unit):
            pair, i = divmod(unit, STREAMS)
            r = work.tile([P, CHUNKS, HALF], F32, tag="r_vector", bufs=2)
            for j in range(CHUNKS):
                nc.vector.scalar_tensor_tensor(
                    out=r[:, j, :],
                    in0=maps[pair][i][:, j, :],
                    scalar=gate_column(unit, j),
                    in1=maps[pair][1 - i][:, j, :],
                    op0=ALU.mult,
                    op1=ALU.add,
                )
            r_of[unit] = r

        def make_r_in_pieces(unit, piece):
            pair, i = divmod(unit, STREAMS)
            if piece == 0:
                r = work.tile([P, CHUNKS, HALF], F32, tag="r_pieces", bufs=3)
                r_of[unit] = r
            j = piece % CHUNKS
            if piece < CHUNKS:
                nc.scalar.activation(
                    out=r_of[unit][:, j, :], in_=maps[pair][i][:, j, :], func=ACT.Copy, scale=gate_column(unit, j)
                )
            else:
                nc.gpsimd.tensor_tensor(
                    out=r_of[unit][:, j, :], in0=r_of[unit][:, j, :], in1=maps[pair][1 - i][:, j, :], op=ALU.add
                )

        def transpose_r(t):
            unit, b = divmod(t, BLOCKS)
            rT = psum.tile([P, D], F32, tag="rT", bufs=4)
            for j in range(CHUNKS):
                nc.tensor.transpose(rT[:, j * P : (j + 1) * P], r_of[unit][:, j, b * P : (b + 1) * P], ident_f32[:])
            rT_of[t] = rT

        def first_exp(t):
            e = work.tile([P, D], F32, tag="e", bufs=3)
            nc.scalar.activation(out=e[:], in_=rT_of[t][:], func=ACT.Exp)
            e_of[t] = e

        def take_max(t):
            neg_max = stats.tile([P, 1], F32, tag="neg_max")
            nc.vector.tensor_reduce(out=neg_max[:], in_=e_of[t][:], axis=mybir.AxisListType.X, op=ALU.max, negate=True)
            neg_max_of[t] = neg_max

        def second_exp(t):
            sum_e = stats.tile([P, 1], F32, tag="sum_e")
            nc.scalar.activation(
                out=e_of[t][:], in_=e_of[t][:], func=ACT.Exp, bias=neg_max_of[t][:], accum_out=sum_e[:]
            )
            sum_e_of[t] = sum_e

        def invert_sum(t):
            inv = stats.tile([P, 1], F32, tag="inv")
            nc.vector.reciprocal(out=inv[:], in_=sum_e_of[t][:])
            inv_of[t] = inv

        def weighted_mean(t):
            s = stats.tile([P, 1], F32, tag="s")
            nc.vector.scalar_tensor_tensor(
                out=e_of[t][:],
                in0=e_of[t][:],
                scalar=inv_of[t][:],
                in1=rT_of[t][:],
                op0=ALU.mult,
                op1=ALU.mult,
                accum_out=s[:],
            )
            s_of[t] = s

        def transpose_own(t):
            unit, b = divmod(t, BLOCKS)
            pair, i = divmod(unit, STREAMS)
            xT = psum.tile([P, D], BF16, tag="xT", bufs=2)
            for j in range(CHUNKS):
                nc.tensor.transpose(xT[:, j * P : (j + 1) * P], maps[pair][i][:, j, b * P : (b + 1) * P], ident_bf16[:])
            xT_of[t] = xT

        def scale_own(t):
            scaled = work.tile([P, D], F32, tag="scaled", bufs=2)
            nc.scalar.activation(out=scaled[:], in_=xT_of[t][:], func=ACT.Copy, scale=s_of[t][:])
            scaled_of[t] = scaled

        def transpose_back(t):
            back = psum.tile([P, CHUNKS, P], F32, tag="back", bufs=2)
            for j in range(CHUNKS):
                nc.tensor.transpose(back[:, j, :], scaled_of[t][:, j * P : (j + 1) * P], ident_f32[:])
            back_of[t] = back

        def add_rest(t):
            unit, b = divmod(t, BLOCKS)
            if b == 0:
                grouped = work.tile([P, HALF, PACK], BF16, tag="grouped", bufs=2, align_bytes=64)
                grouped_of[unit] = grouped
            nc.vector.tensor_tensor(
                out=grouped_of[unit][:, b * P : (b + 1) * P, :],
                in0=back_of[t][:].rearrange("p j w -> p w j"),
                in1=u_of[unit][:, :, b * P : (b + 1) * P].rearrange("p j w -> p w j"),
                op=ALU.add,
            )

        def quantise(unit):
            pair, i = divmod(unit, STREAMS)
            if i == 0:
                codes = work.tile([P, STREAMS, HALF], U32, tag="codes", bufs=2, align_bytes=64)
                scales = work.tile([P, STREAMS, HALF], U8, tag="scales", bufs=2, align_bytes=64)
                codes_of[pair], scales_of[pair] = codes, scales
            nc.vector.quantize_mx(
                out=codes_of[pair][:, i, :].bitcast(FP8X4),
                scales=scales_of[pair][:, i, :],
                in_=grouped_of[unit][:].rearrange("p w t -> p (w t)"),
            )

        def project(pair, quarter):
            acc = psum.tile([P, 2, QUARTER], F32, tag="rT", bufs=4)
            q_cols = slice(quarter * QUARTER, (quarter + 1) * QUARTER)
            for w in range(2):
                for i in range(STREAMS):
                    w_cols = slice((w * STREAMS + i) * OUT, (w * STREAMS + i + 1) * OUT)
                    nc.tensor.matmul_mx(
                        out=acc[:, w, :],
                        lhsT=w_codes[:, w_cols].bitcast(FP8X4),
                        lhsT_scale=w_scales[:, w_cols],
                        rhs=codes_of[pair][:, i, q_cols].bitcast(FP8X4),
                        rhs_scale=scales_of[pair][:, i, q_cols],
                        start=(i == 0),
                        stop=(i == STREAMS - 1),
                    )
            acc_of[(pair, quarter)] = acc

        def store(pair, quarter):
            n, half = divmod(pair, POS // HALF)
            if quarter == 0:
                result = work.tile([P, 2, HALF], F32, tag="result", bufs=2)
                result_of[pair] = result
            q_cols = slice(quarter * QUARTER, (quarter + 1) * QUARTER)
            for w in range(2):
                nc.scalar.activation(
                    out=result_of[pair][:, w, q_cols],
                    in_=acc_of[(pair, quarter)][:, w, :],
                    func=ACT.Identity,
                    bias=bias[:, w : w + 1],
                )
            if quarter == 1:
                for w in range(2):
                    nc.sync.dma_start(out=out_views[w][n, :, half * HALF : (half + 1) * HALF], in_=result_of[pair][:, w, :])

        with tc.manual_schedule():
            for step in range(-LOAD_LEAD, TILES + 8):
                if (step + LOAD_LEAD) % 8 == 0 and (step + LOAD_LEAD) // 8 < PAIRS:
                    load_pair((step + LOAD_LEAD) // 8)
                if 0 <= step + R_LEAD < TILES:
                    make_r_in_pieces((step + R_LEAD) // 8 * STREAMS + 1, (step + R_LEAD) % 8)
                if 0 <= step + U_LEAD < TILES:
                    make_u((step + U_LEAD) // BLOCKS, (step + U_LEAD) % BLOCKS)

                if 0 <= step + 1 < TILES:
                    transpose_r(step + 1)
                if 0 <= step - 2 < TILES:
                    transpose_own(step - 2)
                if 0 <= step < TILES:
                    first_exp(step)
                    take_max(step)
                if step % BLOCKS == 0 and 0 <= step // BLOCKS - 2 < UNITS:
                    quantise(step // BLOCKS - 2)
                if 0 <= step - 1 < TILES:
                    second_exp(step - 1)
                    invert_sum(step - 1)
                if 0 <= step - 3 < TILES:
                    scale_own(step - 3)
                    transpose_back(step - 3)
                if 0 <= step - 4 < TILES:
                    add_rest(step - 4)
                if 0 <= step - 1 < TILES:
                    weighted_mean(step - 1)
                if step % 8 == 5 and 0 <= step // 8 + 1 < PAIRS:
                    make_r_on_vector((step // 8 + 1) * STREAMS)
                if step >= 12 and step % 8 == 4:
                    project(step // 8 - 1, 0)
                if step >= 12 and step % 8 == 5:
                    store(step // 8 - 1, 0)
                if step >= 12 and step % 8 == 6:
                    project(step // 8 - 1, 1)
                if step >= 12 and step % 8 == 7:
                    store(step // 8 - 1, 1)
